import numpy as np
import ml_dtypes


def mxq(x, axis, fmt="e4m3"):
    dtype, down = {"e4m3": (ml_dtypes.float8_e4m3fn, 7), "e5m2": (ml_dtypes.float8_e5m2, 14)}[fmt]
    v = np.moveaxis(np.asarray(x, np.float32).astype(ml_dtypes.bfloat16).astype(np.float64), axis, -1)
    blocks = v.reshape(v.shape[:-1] + (-1, 32))
    amax = np.abs(blocks).max(-1, keepdims=True)
    byte = np.maximum(np.where(amax > 0, np.frexp(amax)[1] - 1 + 127, 0) - down, 1)
    scale = np.exp2(byte - 127.0)
    codes = (blocks / scale).astype(np.float32).astype(dtype).astype(np.float64)
    return np.moveaxis((codes * scale).reshape(v.shape), -1, axis)


WIDE = False


def mx_kscale(k):
    if not WIDE:
        return np.ones(k)
    levels = np.array([30, -30])
    if k % 512:
        return np.exp2(np.random.permutation(np.resize(levels, k // 32))).repeat(32)
    a = np.empty((k // 512, 16))
    for p in range(k // 512):
        a[p, :8] = np.random.permutation(np.resize(levels, 8))
        for g in range(8):
            far = levels[np.abs(levels - a[p, g]) >= 10]
            a[p, g + 8] = far[np.random.randint(len(far))]
    return np.exp2(a.ravel()).repeat(32)


BF16 = ml_dtypes.bfloat16


def bf(x):
    return np.asarray(x, np.float32).astype(BF16)


def f64(x):
    return np.asarray(x).astype(np.float64)


B, T, D, H, KVH, HD = 2, 512, 2048, 16, 4, 128
HALF = HD // 2
EPS = 1e-6
ROPE_BASE = 10000.0


def zc_rmsnorm(x, scale):
    rms = np.sqrt(np.mean(x ** 2, axis=-1, keepdims=True) + EPS)
    return (1.0 + scale) * x / rms


def apply_rope(x, cos, sin):
    t = x.shape[2]
    c = cos[:t][None, None, :, :]
    s = sin[:t][None, None, :, :]
    x1, x2 = x[..., :HALF], x[..., HALF:]
    return np.concatenate([x1 * c - x2 * s, x2 * c + x1 * s], axis=-1)


def setup_inputs():
    s = mx_kscale(D)
    inv_freq = 1.0 / (ROPE_BASE ** (np.arange(0, HALF) / HALF))
    ang = np.arange(T)[:, None] * inv_freq[None, :]
    return {"kv_input": bf(np.random.standard_normal((B, T, D)) * s),
            "Wk": bf(np.random.standard_normal((D, KVH * HD)) / np.sqrt(D) / s[:, None]),
            "Wv": bf(np.random.standard_normal((D, KVH * HD)) / np.sqrt(D) / s[:, None]),
            "k_scale": bf(np.random.standard_normal(HD) * 0.2),
            "cos": bf(np.cos(ang)), "sin": bf(np.sin(ang))}


def reference(kv_input, Wk, Wv, k_scale, cos, sin):
    b = kv_input.shape[0]
    xq = mxq(f64(kv_input), 2, "e5m2")
    k = (xq @ mxq(f64(Wk), 0, "e5m2")).reshape(b, -1, KVH, HD).transpose(0, 2, 1, 3)
    v = (xq @ mxq(f64(Wv), 0, "e5m2")).reshape(b, -1, KVH, HD).transpose(0, 2, 1, 3)
    k = zc_rmsnorm(k, f64(k_scale))
    rep = H // KVH
    k = np.repeat(k, rep, axis=1)
    v = np.repeat(v, rep, axis=1)
    k = apply_rope(k, f64(cos), f64(sin))
    return k, v

@@ -1,0 +1,276 @@
+from contextlib import ExitStack
+
+import concourse.mybir as mybir
+from concourse.masks import make_identity
+
+F32 = mybir.dt.float32
+BF16 = mybir.dt.bfloat16
+U32 = mybir.dt.uint32
+U8 = mybir.dt.uint8
+E5X4 = mybir.dt.float8_e5m2_x4
+ACT = mybir.ActivationFunctionType
+ALU = mybir.AluOpType
+
+B, T, D = 2, 512, 2048
+G, HD, R = 4, 128, 4
+HALF = HD // 2
+EPS = 1e-6
+P = 128
+J = T // P
+K_PASS = 4 * P
+NPASS = D // K_PASS
+NW = G * HD
+W_SPLIT = 352
+
+FLOPS = 2 * B * T * D * 2 * NW
+
+
+def tile_multiheadattention_pb_kernel(tc, kv_input, Wk, Wv, k_scale, cos, sin, out_0, out_1):
+    nc = tc.nc
+    weights = {"k": Wk, "v": Wv}
+
+    with ExitStack() as ctx:
+        keep = ctx.enter_context(tc.tile_pool(name="keep", bufs=1))
+        work = ctx.enter_context(tc.tile_pool(name="work", bufs=3))
+        psum = ctx.enter_context(tc.psum_pool(name="psum", bufs=4))
+        ctx.enter_context(tc.manual_schedule())
+
+        x_raw, x_codes, x_scales = {}, {}, {}
+        for b in range(B):
+            for j in range(J):
+                x_raw[b, j] = keep.tile([P, D], BF16, name="x_raw%d%d" % (b, j))
+                x_codes[b, j] = keep.tile([P, NPASS * P], U32, name="x_codes%d%d" % (b, j), align_bytes=64)
+                x_scales[b, j] = keep.tile([P, NPASS * P], U8, name="x_scales%d%d" % (b, j), align_bytes=64)
+        w_raw, w_codes, w_scales = {}, {}, {}
+        for m in ("v", "k"):
+            for c in range(NPASS):
+                w_raw[m, c] = keep.tile([P, 4, NW], BF16, name="w_raw%s%d" % (m, c))
+                w_codes[m, c] = keep.tile([P, NW], U32, name="w_codes%s%d" % (m, c), align_bytes=64)
+                w_scales[m, c] = keep.tile([P, NW], U8, name="w_scales%s%d" % (m, c), align_bytes=64)
+        v_sb, k_sb = {}, {}
+        for b in range(B):
+            v_sb[b] = keep.tile([P, G, J * HD], F32, name="v_sb%d" % b)
+            k_sb[b] = keep.tile([P, G, J * HD], F32, name="k_sb%d" % b)
+
+        one_col = keep.tile([P, 1], F32, name="one_col")
+        eps_col = keep.tile([P, 1], F32, name="eps_col")
+        warm = keep.tile([P, 1], F32, name="warm")
+        ones = keep.tile([P, P], BF16, name="ones")
+        ks_row = keep.tile([P, HD], BF16, name="ks_row")
+        ident = keep.tile([P, P], F32, name="ident")
+        cos_sb = keep.tile([P, J, HALF], BF16, name="cos_sb")
+        sin_sb = keep.tile([P, J, HALF], BF16, name="sin_sb")
+        gain = keep.tile([P, HD], F32, name="gain")
+        gain_s = keep.tile([P, HD], F32, name="gain_s")
+        tab_a = keep.tile([P, J, HD], F32, name="tab_a")
+        tab_b = keep.tile([P, J, HD], F32, name="tab_b")
+
+        nc.vector.memset(one_col[:], 1.0)
+        nc.scalar.activation(out=warm[:], in_=one_col[:], func=ACT.Sqrt)
+        make_identity(nc, ident[:])
+        nc.vector.tensor_scalar(out=eps_col[:], in0=one_col[:], scalar1=0.0, scalar2=EPS, op0=ALU.mult, op1=ALU.add)
+        nc.vector.memset(ones[:], 1.0)
+        nc.vector.memset(ks_row[:], 0.0)
+
+        def load_x(b, j):
+            nc.sync.dma_start(out=x_raw[b, j][:], in_=kv_input[b].rearrange("(p j) k -> p j k", j=J)[:, j, :])
+
+        def load_w(m, c):
+            rows = weights[m][c * K_PASS : (c + 1) * K_PASS, :]
+            nc.sync.dma_start(out=w_raw[m, c][:], in_=rows.rearrange("(p j) w -> p j w", j=4))
+
+        for s in range(4):
+            load_x(0, s)
+            load_w("v", s)
+        nc.sync.dma_start(out=ks_row[0:1, :], in_=k_scale.rearrange("(o d) -> o d", o=1))
+        nc.sync.dma_start(out=cos_sb[:], in_=cos.rearrange("(p j) c -> p j c", j=J))
+        nc.sync.dma_start(out=sin_sb[:], in_=sin.rearrange("(p j) c -> p j c", j=J))
+        for s in range(4):
+            load_x(1, s)
+            load_w("k", s)
+
+        def transpose_x(b, j):
+            words = x_raw[b, j][:].bitcast(F32)
+            banks = []
+            for h in range(2):
+                xt = psum.tile([P, 4, P], F32, name="xt%d%d%d" % (b, j, h), tag="xt")
+                for i in range(4):
+                    c, u = 2 * h + i // 2, i % 2
+                    nc.tensor.transpose(
+                        out=xt[:, i, :], in_=words[:, 256 * c + u : 256 * (c + 1) : 2], identity=ident[:]
+                    )
+                banks.append(xt)
+            return banks
+
+        def copy_x(b, j, banks):
+            grp = work.tile([P, D], BF16, name="x_grp%d%d" % (b, j), tag="x_grp", align_bytes=64)
+            grp_words = grp[:].bitcast(F32)
+            for h in range(2):
+                nc.scalar.copy(
+                    out=grp_words[:, 512 * h : 512 * (h + 1)].rearrange("p (c r u) -> p c r u", c=2, u=2),
+                    in_=banks[h][:].rearrange("p (c u) r -> p c r u", u=2),
+                )
+            return grp
+
+        def quantize_x(b, j, grp):
+            nc.vector.quantize_mx(out=x_codes[b, j][:].bitcast(E5X4), scales=x_scales[b, j][:], in_=grp[:])
+
+        def copy_w(m, c):
+            grp = work.tile([P, NW, 4], BF16, name="w_grp%s%d" % (m, c), tag="w_grp", align_bytes=64)
+            src = w_raw[m, c][:].rearrange("p j w -> p w j")
+            nc.vector.tensor_copy(out=grp[:, :W_SPLIT, :], in_=src[:, :W_SPLIT, :])
+            nc.scalar.copy(out=grp[:, W_SPLIT:, :], in_=src[:, W_SPLIT:, :])
+            return grp
+
+        def quantize_w(m, c, grp):
+            nc.vector.quantize_mx(
+                out=w_codes[m, c][:].bitcast(E5X4),
+                scales=w_scales[m, c][:],
+                in_=grp[:].rearrange("p w j -> p (w j)"),
+            )
+
+        def new_acc(m, b, j):
+            return psum.tile([P, NW], F32, name="acc%s%d%d" % (m, b, j), tag="acc")
+
+        def mm(acc, m, b, j, c):
+            cols = slice(c * P, (c + 1) * P)
+            nc.tensor.matmul_mx(
+                out=acc[:],
+                lhsT=x_codes[b, j][:, cols].bitcast(E5X4),
+                lhsT_scale=x_scales[b, j][:, cols],
+                rhs=w_codes[m, c][:].bitcast(E5X4),
+                rhs_scale=w_scales[m, c][:],
+                start=(c == 0),
+                stop=(c == NPASS - 1),
+            )
+
+        def evacuate_v(acc, b, j):
+            dst = v_sb[b][:, :, j * HD : (j + 1) * HD]
+            src = acc[:].rearrange("p (g d) -> p g d", g=G)
+            if j % 2 == 0:
+                nc.vector.tensor_copy(out=dst, in_=src)
+            else:
+                nc.scalar.copy(out=dst, in_=src)
+
+        def store(dst, b, src):
+            view = dst[b].rearrange("(g r) (p j) d -> r p g (j d)", r=R, j=J)
+            for r in range(R):
+                nc.sync.dma_start(out=view[r], in_=src[:])
+
+        acc_v = {}
+        banks = transpose_x(0, 0)
+        for s in range(4):
+            x_grp = copy_x(0, s, banks)
+            w_grp = copy_w("v", s)
+            banks = transpose_x(0, s + 1) if s < 3 else transpose_x(1, 0)
+            quantize_x(0, s, x_grp)
+            quantize_w("v", s, w_grp)
+            acc_v[s] = new_acc("v", 0, s)
+            for j in range(s):
+                mm(acc_v[j], "v", 0, j, s)
+            for c in range(s + 1):
+                mm(acc_v[s], "v", 0, s, c)
+
+        last = None
+        for s in range(4):
+            x_grp = copy_x(1, s, banks)
+            w_grp = copy_w("k", s)
+            if s < 3:
+                banks = transpose_x(1, s + 1)
+            if s == 0:
+                for j in range(J):
+                    evacuate_v(acc_v[j], 0, j)
+                store(out_1, 0, v_sb[0])
+            else:
+                evacuate_v(last, 1, s - 1)
+            quantize_x(1, s, x_grp)
+            quantize_w("k", s, w_grp)
+            last = new_acc("v", 1, s)
+            for c in range(NPASS):
+                mm(last, "v", 1, s, c)
+        evacuate_v(last, 1, 3)
+        store(out_1, 1, v_sb[1])
+
+        acc_k, rstd, xn, yz = {}, {}, {}, {}
+
+        def mm_k(i):
+            acc_k[i] = new_acc("k", i // J, i % J)
+            for c in range(NPASS):
+                mm(acc_k[i], "k", i // J, i % J, c)
+
+        def stats(i):
+            ss = work.tile([P, G], F32, name="ss%d" % i, tag="ss", bufs=4)
+            rms = work.tile([P, G], F32, name="rms%d" % i, tag="rms", bufs=4)
+            rstd[i] = work.tile([P, G], F32, name="rstd%d" % i, tag="rstd", bufs=4)
+            for g in range(G):
+                junk = work.tile([P, HD], BF16, name="junk%d%d" % (i, g), tag="junk", bufs=2)
+                nc.scalar.activation(
+                    out=junk[:], in_=acc_k[i][:, g * HD : (g + 1) * HD], func=ACT.Square, accum_out=ss[:, g : g + 1]
+                )
+            nc.scalar.activation(out=rms[:], in_=ss[:], func=ACT.Sqrt, bias=eps_col[:], scale=1.0 / HD)
+            nc.vector.reciprocal(out=rstd[i][:], in_=rms[:])
+
+        def normalise(i):
+            xn[i] = work.tile([P, G, HD], F32, name="xn%d" % i, tag="xn")
+            for g in range(G):
+                nc.scalar.activation(
+                    out=xn[i][:, g, :],
+                    in_=acc_k[i][:, g * HD : (g + 1) * HD],
+                    func=ACT.Copy,
+                    scale=rstd[i][:, g : g + 1],
+                )
+
+        def rope_mul(i):
+            j = i % J
+            y = work.tile([P, G, HD], F32, name="y%d" % i, tag="y")
+            z = work.tile([P, G, HD], F32, name="z%d" % i, tag="z")
+            nc.vector.tensor_tensor(
+                out=y[:], in0=xn[i][:], in1=tab_a[:, j, :].unsqueeze(1).to_broadcast([P, G, HD]), op=ALU.mult
+            )
+            nc.vector.tensor_tensor(
+                out=z[:], in0=xn[i][:], in1=tab_b[:, j, :].unsqueeze(1).to_broadcast([P, G, HD]), op=ALU.mult
+            )
+            yz[i] = (y, z)
+
+        def rope_add(i):
+            b, j = i // J, i % J
+            y, z = yz[i]
+            lo, mid, hi = j * HD, j * HD + HALF, (j + 1) * HD
+            nc.vector.tensor_tensor(out=k_sb[b][:, :, lo:mid], in0=y[:, :, :HALF], in1=z[:, :, HALF:], op=ALU.add)
+            nc.vector.tensor_tensor(out=k_sb[b][:, :, mid:hi], in0=y[:, :, HALF:], in1=z[:, :, :HALF], op=ALU.add)
+
+        mm_k(0)
+        mm_k(1)
+        stats(0)
+
+        ks_ps = psum.tile([P, 4, P], F32, name="ks_ps", tag="xt")
+        nc.tensor.matmul(out=ks_ps[:, 0, :], lhsT=ones[:], rhs=ks_row[:], start=True, stop=True)
+        nc.vector.tensor_scalar(out=gain[:], in0=ks_ps[:, 0, :], scalar1=1.0, scalar2=None, op0=ALU.add)
+        nc.vector.tensor_scalar(out=gain_s[:, :HALF], in0=ks_ps[:, 0, :HALF], scalar1=1.0, scalar2=None, op0=ALU.add)
+        nc.vector.tensor_scalar(
+            out=gain_s[:, HALF:], in0=ks_ps[:, 0, HALF:], scalar1=-1.0, scalar2=-1.0, op0=ALU.mult, op1=ALU.add
+        )
+        for tab, gn, trig in ((tab_a, gain, cos_sb), (tab_b, gain_s, sin_sb)):
+            nc.vector.tensor_tensor(
+                out=tab[:].rearrange("p j (h c) -> p j h c", h=2),
+                in0=gn[:].rearrange("p (h c) -> p h c", h=2).unsqueeze(1).to_broadcast([P, J, 2, HALF]),
+                in1=trig[:].unsqueeze(2).to_broadcast([P, J, 2, HALF]),
+                op=ALU.mult,
+            )
+
+        stats(1)
+        mm_k(2)
+        mm_k(3)
+        for i in range(B * J):
+            normalise(i)
+            if i + 4 < B * J:
+                mm_k(i + 4)
+            rope_mul(i)
+            if i >= 1:
+                rope_add(i - 1)
+            if i == J:
+                store(out_0, 0, k_sb[0])
+            if i + 2 < B * J:
+                stats(i + 2)
+        rope_add(B * J - 1)
+        store(out_0, 1, k_sb[1])

@@ -20,7 +20,8 @@ J = T // P
 K_PASS = 4 * P
 NPASS = D // K_PASS
 NW = G * HD
-W_SPLIT = 352
+W_SPLIT = {"v": 336, "k": 336}
+V_ON_VECTOR = ((0, 0), (0, 2))
 
 FLOPS = 2 * B * T * D * 2 * NW
 
@@ -65,12 +66,12 @@ def tile_multiheadattention_pb_kernel(tc, kv_input, Wk, Wv, k_scale, cos, sin, o
         tab_a = keep.tile([P, J, HD], F32, name="tab_a")
         tab_b = keep.tile([P, J, HD], F32, name="tab_b")
 
+        nc.vector.memset(ks_row[:], 0.0)
         nc.vector.memset(one_col[:], 1.0)
         nc.scalar.activation(out=warm[:], in_=one_col[:], func=ACT.Sqrt)
         make_identity(nc, ident[:])
-        nc.vector.tensor_scalar(out=eps_col[:], in0=one_col[:], scalar1=0.0, scalar2=EPS, op0=ALU.mult, op1=ALU.add)
         nc.vector.memset(ones[:], 1.0)
-        nc.vector.memset(ks_row[:], 0.0)
+        nc.vector.tensor_scalar(out=eps_col[:], in0=one_col[:], scalar1=0.0, scalar2=EPS, op0=ALU.mult, op1=ALU.add)
 
         def load_x(b, j):
             nc.sync.dma_start(out=x_raw[b, j][:], in_=kv_input[b].rearrange("(p j) k -> p j k", j=J)[:, j, :])
@@ -81,12 +82,14 @@ def tile_multiheadattention_pb_kernel(tc, kv_input, Wk, Wv, k_scale, cos, sin, o
 
         for s in range(4):
             load_x(0, s)
+            if s == 0:
+                nc.sync.dma_start(out=ks_row[0:1, :], in_=k_scale.rearrange("(o d) -> o d", o=1))
             load_w("v", s)
-        nc.sync.dma_start(out=ks_row[0:1, :], in_=k_scale.rearrange("(o d) -> o d", o=1))
         nc.sync.dma_start(out=cos_sb[:], in_=cos.rearrange("(p j) c -> p j c", j=J))
         nc.sync.dma_start(out=sin_sb[:], in_=sin.rearrange("(p j) c -> p j c", j=J))
         for s in range(4):
             load_x(1, s)
+        for s in range(4):
             load_w("k", s)
 
         def transpose_x(b, j):
@@ -118,8 +121,8 @@ def tile_multiheadattention_pb_kernel(tc, kv_input, Wk, Wv, k_scale, cos, sin, o
         def copy_w(m, c):
             grp = work.tile([P, NW, 4], BF16, name="w_grp%s%d" % (m, c), tag="w_grp", align_bytes=64)
             src = w_raw[m, c][:].rearrange("p j w -> p w j")
-            nc.vector.tensor_copy(out=grp[:, :W_SPLIT, :], in_=src[:, :W_SPLIT, :])
-            nc.scalar.copy(out=grp[:, W_SPLIT:, :], in_=src[:, W_SPLIT:, :])
+            nc.vector.tensor_copy(out=grp[:, : W_SPLIT[m], :], in_=src[:, : W_SPLIT[m], :])
+            nc.scalar.copy(out=grp[:, W_SPLIT[m] :, :], in_=src[:, W_SPLIT[m] :, :])
             return grp
 
         def quantize_w(m, c, grp):
@@ -128,9 +131,6 @@ def tile_multiheadattention_pb_kernel(tc, kv_input, Wk, Wv, k_scale, cos, sin, o
                 scales=w_scales[m, c][:],
                 in_=grp[:].rearrange("p w j -> p (w j)"),
             )
-
-        def new_acc(m, b, j):
-            return psum.tile([P, NW], F32, name="acc%s%d%d" % (m, b, j), tag="acc")
 
         def mm(acc, m, b, j, c):
             cols = slice(c * P, (c + 1) * P)
@@ -147,109 +147,57 @@ def tile_multiheadattention_pb_kernel(tc, kv_input, Wk, Wv, k_scale, cos, sin, o
         def evacuate_v(acc, b, j):
             dst = v_sb[b][:, :, j * HD : (j + 1) * HD]
             src = acc[:].rearrange("p (g d) -> p g d", g=G)
-            if j % 2 == 0:
+            if (b, j) in V_ON_VECTOR:
                 nc.vector.tensor_copy(out=dst, in_=src)
             else:
                 nc.scalar.copy(out=dst, in_=src)
 
-        def store(dst, b, src):
-            view = dst[b].rearrange("(g r) (p j) d -> r p g (j d)", r=R, j=J)
+        def store_v(b):
+            view = out_1[b].rearrange("(g r) (p j) d -> r p g (j d)", r=R, j=J)
             for r in range(R):
-                nc.sync.dma_start(out=view[r], in_=src[:])
+                nc.sync.dma_start(out=view[r], in_=v_sb[b][:])
+
+        def store_k(b, g):
+            heads = out_0[b, g * R : (g + 1) * R].rearrange("r (p j) d -> p r (j d)", j=J)
+            nc.sync.dma_start(out=heads, in_=k_sb[b][:, g, :].unsqueeze(1).to_broadcast([P, R, J * HD]))
+
+        ks_ps = psum.tile([P, NW], F32, name="ks_ps", tag="xt")
+        nc.tensor.matmul(out=ks_ps[:, :HD], lhsT=ones[:], rhs=ks_row[:], start=True, stop=True)
+        nc.vector.tensor_scalar(out=gain[:], in0=ks_ps[:, :HD], scalar1=1.0, scalar2=None, op0=ALU.add)
+        nc.vector.tensor_scalar(out=gain_s[:, :HALF], in0=ks_ps[:, :HALF], scalar1=1.0, scalar2=None, op0=ALU.add)
+        nc.vector.tensor_scalar(
+            out=gain_s[:, HALF:], in0=ks_ps[:, HALF:HD], scalar1=-1.0, scalar2=-1.0, op0=ALU.mult, op1=ALU.add
+        )
 
         acc_v = {}
-        banks = transpose_x(0, 0)
+        banks = {}
+        banks[0, 0] = transpose_x(0, 0)
         for s in range(4):
-            x_grp = copy_x(0, s, banks)
+            x_grp = copy_x(0, s, banks[0, s])
             w_grp = copy_w("v", s)
-            banks = transpose_x(0, s + 1) if s < 3 else transpose_x(1, 0)
+            if s < 3:
+                banks[0, s + 1] = transpose_x(0, s + 1)
             quantize_x(0, s, x_grp)
             quantize_w("v", s, w_grp)
-            acc_v[s] = new_acc("v", 0, s)
-            for j in range(s):
-                mm(acc_v[j], "v", 0, j, s)
-            for c in range(s + 1):
-                mm(acc_v[s], "v", 0, s, c)
+            acc_v[0, s] = psum.tile([P, NW], F32, name="acc_v0%d" % s, tag="acc")
+            for c in range(s):
+                mm(acc_v[0, s], "v", 0, s, c)
+            for j in range(s + 1):
+                mm(acc_v[0, j], "v", 0, j, s)
 
-        last = None
-        for s in range(4):
-            x_grp = copy_x(1, s, banks)
-            w_grp = copy_w("k", s)
-            if s < 3:
-                banks = transpose_x(1, s + 1)
-            if s == 0:
-                for j in range(J):
-                    evacuate_v(acc_v[j], 0, j)
-                store(out_1, 0, v_sb[0])
-            else:
-                evacuate_v(last, 1, s - 1)
-            quantize_x(1, s, x_grp)
-            quantize_w("k", s, w_grp)
-            last = new_acc("v", 1, s)
+        def mm_v1(s):
+            acc_v[1, s] = psum.tile([P, NW], F32, name="acc_v1%d" % s, tag="acc")
             for c in range(NPASS):
-                mm(last, "v", 1, s, c)
-        evacuate_v(last, 1, 3)
-        store(out_1, 1, v_sb[1])
+                mm(acc_v[1, s], "v", 1, s, c)
 
-        acc_k, rstd, xn, yz = {}, {}, {}, {}
+        x_grps, w_grps = {}, {}
+        banks[1, 0] = transpose_x(1, 0)
+        banks[1, 1] = transpose_x(1, 1)
+        for j in range(J):
+            evacuate_v(acc_v[0, j], 0, j)
+        store_v(0)
+        x_grps[0] = copy_x(1, 0, banks[1, 0])
 
-        def mm_k(i):
-            acc_k[i] = new_acc("k", i // J, i % J)
-            for c in range(NPASS):
-                mm(acc_k[i], "k", i // J, i % J, c)
-
-        def stats(i):
-            ss = work.tile([P, G], F32, name="ss%d" % i, tag="ss", bufs=4)
-            rms = work.tile([P, G], F32, name="rms%d" % i, tag="rms", bufs=4)
-            rstd[i] = work.tile([P, G], F32, name="rstd%d" % i, tag="rstd", bufs=4)
-            for g in range(G):
-                junk = work.tile([P, HD], BF16, name="junk%d%d" % (i, g), tag="junk", bufs=2)
-                nc.scalar.activation(
-                    out=junk[:], in_=acc_k[i][:, g * HD : (g + 1) * HD], func=ACT.Square, accum_out=ss[:, g : g + 1]
-                )
-            nc.scalar.activation(out=rms[:], in_=ss[:], func=ACT.Sqrt, bias=eps_col[:], scale=1.0 / HD)
-            nc.vector.reciprocal(out=rstd[i][:], in_=rms[:])
-
-        def normalise(i):
-            xn[i] = work.tile([P, G, HD], F32, name="xn%d" % i, tag="xn")
-            for g in range(G):
-                nc.scalar.activation(
-                    out=xn[i][:, g, :],
-                    in_=acc_k[i][:, g * HD : (g + 1) * HD],
-                    func=ACT.Copy,
-                    scale=rstd[i][:, g : g + 1],
-                )
-
-        def rope_mul(i):
-            j = i % J
-            y = work.tile([P, G, HD], F32, name="y%d" % i, tag="y")
-            z = work.tile([P, G, HD], F32, name="z%d" % i, tag="z")
-            nc.vector.tensor_tensor(
-                out=y[:], in0=xn[i][:], in1=tab_a[:, j, :].unsqueeze(1).to_broadcast([P, G, HD]), op=ALU.mult
-            )
-            nc.vector.tensor_tensor(
-                out=z[:], in0=xn[i][:], in1=tab_b[:, j, :].unsqueeze(1).to_broadcast([P, G, HD]), op=ALU.mult
-            )
-            yz[i] = (y, z)
-
-        def rope_add(i):
-            b, j = i // J, i % J
-            y, z = yz[i]
-            lo, mid, hi = j * HD, j * HD + HALF, (j + 1) * HD
-            nc.vector.tensor_tensor(out=k_sb[b][:, :, lo:mid], in0=y[:, :, :HALF], in1=z[:, :, HALF:], op=ALU.add)
-            nc.vector.tensor_tensor(out=k_sb[b][:, :, mid:hi], in0=y[:, :, HALF:], in1=z[:, :, :HALF], op=ALU.add)
-
-        mm_k(0)
-        mm_k(1)
-        stats(0)
-
-        ks_ps = psum.tile([P, 4, P], F32, name="ks_ps", tag="xt")
-        nc.tensor.matmul(out=ks_ps[:, 0, :], lhsT=ones[:], rhs=ks_row[:], start=True, stop=True)
-        nc.vector.tensor_scalar(out=gain[:], in0=ks_ps[:, 0, :], scalar1=1.0, scalar2=None, op0=ALU.add)
-        nc.vector.tensor_scalar(out=gain_s[:, :HALF], in0=ks_ps[:, 0, :HALF], scalar1=1.0, scalar2=None, op0=ALU.add)
-        nc.vector.tensor_scalar(
-            out=gain_s[:, HALF:], in0=ks_ps[:, 0, HALF:], scalar1=-1.0, scalar2=-1.0, op0=ALU.mult, op1=ALU.add
-        )
         for tab, gn, trig in ((tab_a, gain, cos_sb), (tab_b, gain_s, sin_sb)):
             nc.vector.tensor_tensor(
                 out=tab[:].rearrange("p j (h c) -> p j h c", h=2),
@@ -258,19 +206,98 @@ def tile_multiheadattention_pb_kernel(tc, kv_input, Wk, Wv, k_scale, cos, sin, o
                 op=ALU.mult,
             )
 
+        quantize_x(1, 0, x_grps[0])
+        x_grps[1] = copy_x(1, 1, banks[1, 1])
+        banks[1, 2] = transpose_x(1, 2)
+        mm_v1(0)
+        quantize_x(1, 1, x_grps[1])
+        x_grps[2] = copy_x(1, 2, banks[1, 2])
+        banks[1, 3] = transpose_x(1, 3)
+        mm_v1(1)
+        quantize_x(1, 2, x_grps[2])
+        x_grps[3] = copy_x(1, 3, banks[1, 3])
+        mm_v1(2)
+        evacuate_v(acc_v[1, 0], 1, 0)
+        w_grps[0] = copy_w("k", 0)
+        quantize_x(1, 3, x_grps[3])
+        mm_v1(3)
+        evacuate_v(acc_v[1, 1], 1, 1)
+        w_grps[1] = copy_w("k", 1)
+        quantize_w("k", 0, w_grps[0])
+        evacuate_v(acc_v[1, 2], 1, 2)
+        evacuate_v(acc_v[1, 3], 1, 3)
+        store_v(1)
+        acc_k = {}
+        for j in range(J):
+            acc_k[0, j] = psum.tile([P, NW], F32, name="acc_k0%d" % j, tag="acc")
+            mm(acc_k[0, j], "k", 0, j, 0)
+        for c in range(1, NPASS):
+            if c + 1 < NPASS:
+                w_grps[c + 1] = copy_w("k", c + 1)
+            quantize_w("k", c, w_grps[c])
+            for j in range(J):
+                mm(acc_k[0, j], "k", 0, j, c)
+        for j in range(J):
+            acc_k[1, j] = psum.tile([P, NW], F32, name="acc_k1%d" % j, tag="xt")
+
+        rstd, xn, yz = {}, {}, {}
+
+        def stats(u):
+            b, g = u // G, u % G
+            ss = work.tile([P, J], F32, name="ss%d" % u, tag="ss", bufs=4)
+            rms = work.tile([P, J], F32, name="rms%d" % u, tag="rms", bufs=4)
+            rstd[u] = work.tile([P, J], F32, name="rstd%d" % u, tag="rstd", bufs=4)
+            for j in range(J):
+                junk = work.tile([P, HD], BF16, name="junk%d%d" % (u, j), tag="junk", bufs=2)
+                nc.scalar.activation(
+                    out=junk[:],
+                    in_=acc_k[b, j][:, g * HD : (g + 1) * HD],
+                    func=ACT.Square,
+                    accum_out=ss[:, j : j + 1],
+                )
+            nc.scalar.activation(out=rms[:], in_=ss[:], func=ACT.Sqrt, bias=eps_col[:], scale=1.0 / HD)
+            nc.vector.reciprocal(out=rstd[u][:], in_=rms[:])
+
+        def normalise(u):
+            b, g = u // G, u % G
+            xn[u] = work.tile([P, J, HD], F32, name="xn%d" % u, tag="xn")
+            for j in range(J):
+                nc.scalar.activation(
+                    out=xn[u][:, j, :],
+                    in_=acc_k[b, j][:, g * HD : (g + 1) * HD],
+                    func=ACT.Copy,
+                    scale=rstd[u][:, j : j + 1],
+                )
+
+        def rope_mul(u):
+            y = work.tile([P, J, HD], F32, name="y%d" % u, tag="y")
+            z = work.tile([P, J, HD], F32, name="z%d" % u, tag="z")
+            nc.vector.tensor_tensor(out=y[:], in0=xn[u][:], in1=tab_a[:], op=ALU.mult)
+            nc.vector.tensor_tensor(out=z[:], in0=xn[u][:], in1=tab_b[:], op=ALU.mult)
+            yz[u] = (y, z)
+
+        def rope_add(u):
+            b, g = u // G, u % G
+            y, z = yz[u]
+            dst = k_sb[b][:, g, :].rearrange("p (j d) -> p j d", j=J)
+            nc.vector.tensor_tensor(out=dst[:, :, :HALF], in0=y[:, :, :HALF], in1=z[:, :, HALF:], op=ALU.add)
+            nc.vector.tensor_tensor(out=dst[:, :, HALF:], in0=y[:, :, HALF:], in1=z[:, :, :HALF], op=ALU.add)
+            store_k(b, g)
+
+        stats(0)
+        for j in range(J):
+            for c in range(NPASS):
+                mm(acc_k[1, j], "k", 1, j, c)
+        normalise(0)
+        rope_mul(0)
+        rope_add(0)
         stats(1)
-        mm_k(2)
-        mm_k(3)
-        for i in range(B * J):
-            normalise(i)
-            if i + 4 < B * J:
-                mm_k(i + 4)
-            rope_mul(i)
-            if i >= 1:
-                rope_add(i - 1)
-            if i == J:
-                store(out_0, 0, k_sb[0])
-            if i + 2 < B * J:
-                stats(i + 2)
-        rope_add(B * J - 1)
-        store(out_0, 1, k_sb[1])
+        stats(2)
+        for u in range(1, B * G):
+            normalise(u)
+            rope_mul(u)
+            if u >= 2:
+                rope_add(u - 1)
+            if u + 2 < B * G:
+                stats(u + 2)
+        rope_add(B * G - 1)

@@ -21,7 +21,7 @@ K_PASS = 4 * P
 NPASS = D // K_PASS
 NW = G * HD
 W_SPLIT = {"v": 336, "k": 336}
-V_ON_VECTOR = ((0, 0), (0, 2))
+V_ON_VECTOR = ((0, 0), (0, 2), (1, 2))
 
 FLOPS = 2 * B * T * D * 2 * NW
 
@@ -120,9 +120,11 @@ def tile_multiheadattention_pb_kernel(tc, kv_input, Wk, Wv, k_scale, cos, sin, o
 
         def copy_w(m, c):
             grp = work.tile([P, NW, 4], BF16, name="w_grp%s%d" % (m, c), tag="w_grp", align_bytes=64)
-            src = w_raw[m, c][:].rearrange("p j w -> p w j")
-            nc.vector.tensor_copy(out=grp[:, : W_SPLIT[m], :], in_=src[:, : W_SPLIT[m], :])
-            nc.scalar.copy(out=grp[:, W_SPLIT[m] :, :], in_=src[:, W_SPLIT[m] :, :])
+            dst = grp[:].rearrange("p (c i) j -> p c j i", i=4)
+            src = w_raw[m, c][:].rearrange("p j (c i) -> p c j i", i=4)
+            cut = W_SPLIT[m] // 4
+            nc.vector.tensor_copy(out=dst[:, :cut], in_=src[:, :cut])
+            nc.scalar.copy(out=dst[:, cut:], in_=src[:, cut:])
             return grp
 
         def quantize_w(m, c, grp):
@@ -240,13 +242,12 @@ def tile_multiheadattention_pb_kernel(tc, kv_input, Wk, Wv, k_scale, cos, sin, o
         for j in range(J):
             acc_k[1, j] = psum.tile([P, NW], F32, name="acc_k1%d" % j, tag="xt")
 
-        rstd, xn, yz = {}, {}, {}
+        rms, rstd, xn, yz = {}, {}, {}, {}
 
-        def stats(u):
+        def squares(u):
             b, g = u // G, u % G
             ss = work.tile([P, J], F32, name="ss%d" % u, tag="ss", bufs=4)
-            rms = work.tile([P, J], F32, name="rms%d" % u, tag="rms", bufs=4)
-            rstd[u] = work.tile([P, J], F32, name="rstd%d" % u, tag="rstd", bufs=4)
+            rms[u] = work.tile([P, J], F32, name="rms%d" % u, tag="rms", bufs=4)
             for j in range(J):
                 junk = work.tile([P, HD], BF16, name="junk%d%d" % (u, j), tag="junk", bufs=2)
                 nc.scalar.activation(
@@ -255,8 +256,11 @@ def tile_multiheadattention_pb_kernel(tc, kv_input, Wk, Wv, k_scale, cos, sin, o
                     func=ACT.Square,
                     accum_out=ss[:, j : j + 1],
                 )
-            nc.scalar.activation(out=rms[:], in_=ss[:], func=ACT.Sqrt, bias=eps_col[:], scale=1.0 / HD)
-            nc.vector.reciprocal(out=rstd[u][:], in_=rms[:])
+            nc.scalar.activation(out=rms[u][:], in_=ss[:], func=ACT.Sqrt, bias=eps_col[:], scale=1.0 / HD)
+
+        def recip(u):
+            rstd[u] = work.tile([P, J], F32, name="rstd%d" % u, tag="rstd", bufs=4)
+            nc.vector.reciprocal(out=rstd[u][:], in_=rms[u][:])
 
         def normalise(u):
             b, g = u // G, u % G
@@ -284,20 +288,25 @@ def tile_multiheadattention_pb_kernel(tc, kv_input, Wk, Wv, k_scale, cos, sin, o
             nc.vector.tensor_tensor(out=dst[:, :, HALF:], in0=y[:, :, HALF:], in1=z[:, :, :HALF], op=ALU.add)
             store_k(b, g)
 
-        stats(0)
+        squares(0)
+        recip(0)
         for j in range(J):
             for c in range(NPASS):
                 mm(acc_k[1, j], "k", 1, j, c)
         normalise(0)
+        squares(1)
+        squares(2)
         rope_mul(0)
+        recip(1)
         rope_add(0)
-        stats(1)
-        stats(2)
+        recip(2)
+        normalise(1)
         for u in range(1, B * G):
-            normalise(u)
-            rope_mul(u)
-            if u >= 2:
-                rope_add(u - 1)
             if u + 2 < B * G:
-                stats(u + 2)
-        rope_add(B * G - 1)
+                squares(u + 2)
+            if u + 1 < B * G:
+                normalise(u + 1)
+            rope_mul(u)
+            if u + 2 < B * G:
+                recip(u + 2)
+            rope_add(u)

@@ -22,6 +22,7 @@ NPASS = D // K_PASS
 NW = G * HD
 W_SPLIT = {"v": 336, "k": 336}
 V_ON_VECTOR = ((0, 0), (0, 2), (1, 2))
+N_WARM = 4
 
 FLOPS = 2 * B * T * D * 2 * NW
 
@@ -56,7 +57,7 @@ def tile_multiheadattention_pb_kernel(tc, kv_input, Wk, Wv, k_scale, cos, sin, o
         one_col = keep.tile([P, 1], F32, name="one_col")
         eps_col = keep.tile([P, 1], F32, name="eps_col")
         warm = keep.tile([P, 1], F32, name="warm")
-        ones = keep.tile([P, P], BF16, name="ones")
+        ones = keep.tile([P, NW], BF16, name="ones")
         ks_row = keep.tile([P, HD], BF16, name="ks_row")
         ident = keep.tile([P, P], F32, name="ident")
         cos_sb = keep.tile([P, J, HALF], BF16, name="cos_sb")
@@ -66,11 +67,11 @@ def tile_multiheadattention_pb_kernel(tc, kv_input, Wk, Wv, k_scale, cos, sin, o
         tab_a = keep.tile([P, J, HD], F32, name="tab_a")
         tab_b = keep.tile([P, J, HD], F32, name="tab_b")
 
+        nc.vector.memset(ones[:], 1.0)
         nc.vector.memset(ks_row[:], 0.0)
         nc.vector.memset(one_col[:], 1.0)
         nc.scalar.activation(out=warm[:], in_=one_col[:], func=ACT.Sqrt)
         make_identity(nc, ident[:])
-        nc.vector.memset(ones[:], 1.0)
         nc.vector.tensor_scalar(out=eps_col[:], in0=one_col[:], scalar1=0.0, scalar2=EPS, op0=ALU.mult, op1=ALU.add)
 
         def load_x(b, j):
@@ -163,8 +164,11 @@ def tile_multiheadattention_pb_kernel(tc, kv_input, Wk, Wv, k_scale, cos, sin, o
             heads = out_0[b, g * R : (g + 1) * R].rearrange("r (p j) d -> p r (j d)", j=J)
             nc.sync.dma_start(out=heads, in_=k_sb[b][:, g, :].unsqueeze(1).to_broadcast([P, R, J * HD]))
 
+        warm_ps = psum.tile([P, NW], F32, name="warm_ps", tag="acc")
+        for i in range(N_WARM):
+            nc.tensor.matmul(out=warm_ps[:], lhsT=ones[:, :P], rhs=ones[:], start=True, stop=True)
         ks_ps = psum.tile([P, NW], F32, name="ks_ps", tag="xt")
-        nc.tensor.matmul(out=ks_ps[:, :HD], lhsT=ones[:], rhs=ks_row[:], start=True, stop=True)
+        nc.tensor.matmul(out=ks_ps[:, :HD], lhsT=ones[:, :P], rhs=ks_row[:], start=True, stop=True)
         nc.vector.tensor_scalar(out=gain[:], in0=ks_ps[:, :HD], scalar1=1.0, scalar2=None, op0=ALU.add)
         nc.vector.tensor_scalar(out=gain_s[:, :HALF], in0=ks_ps[:, :HALF], scalar1=1.0, scalar2=None, op0=ALU.add)
         nc.vector.tensor_scalar(

@@ -39,14 +39,14 @@ def tile_multiheadattention_pb_kernel(tc, kv_input, Wk, Wv, k_scale, cos, sin, o
 
         x_raw, x_codes, x_scales = {}, {}, {}
         for b in range(B):
+            x_raw[b] = keep.tile([P, J, D], BF16, name="x_raw%d" % b)
             for j in range(J):
-                x_raw[b, j] = keep.tile([P, D], BF16, name="x_raw%d%d" % (b, j))
                 x_codes[b, j] = keep.tile([P, NPASS * P], U32, name="x_codes%d%d" % (b, j), align_bytes=64)
                 x_scales[b, j] = keep.tile([P, NPASS * P], U8, name="x_scales%d%d" % (b, j), align_bytes=64)
         w_raw, w_codes, w_scales = {}, {}, {}
         for m in ("v", "k"):
+            w_raw[m] = keep.tile([P, NPASS, 4, NW], BF16, name="w_raw%s" % m)
             for c in range(NPASS):
-                w_raw[m, c] = keep.tile([P, 4, NW], BF16, name="w_raw%s%d" % (m, c))
                 w_codes[m, c] = keep.tile([P, NW], U32, name="w_codes%s%d" % (m, c), align_bytes=64)
                 w_scales[m, c] = keep.tile([P, NW], U8, name="w_scales%s%d" % (m, c), align_bytes=64)
         v_sb, k_sb = {}, {}
@@ -74,27 +74,30 @@ def tile_multiheadattention_pb_kernel(tc, kv_input, Wk, Wv, k_scale, cos, sin, o
         make_identity(nc, ident[:])
         nc.vector.tensor_scalar(out=eps_col[:], in0=one_col[:], scalar1=0.0, scalar2=EPS, op0=ALU.mult, op1=ALU.add)
 
-        def load_x(b, j):
-            nc.sync.dma_start(out=x_raw[b, j][:], in_=kv_input[b].rearrange("(p j) k -> p j k", j=J)[:, j, :])
+        def load_x(b, j, n):
+            nc.sync.dma_start(
+                out=x_raw[b][:, j : j + n, :], in_=kv_input[b].rearrange("(p j) k -> p j k", j=J)[:, j : j + n, :]
+            )
 
-        def load_w(m, c):
-            rows = weights[m][c * K_PASS : (c + 1) * K_PASS, :]
-            nc.sync.dma_start(out=w_raw[m, c][:], in_=rows.rearrange("(p j) w -> p j w", j=4))
+        def load_w(m, c, n):
+            rows = weights[m][c * K_PASS : (c + n) * K_PASS, :]
+            nc.sync.dma_start(
+                out=w_raw[m][:, c : c + n, :, :].rearrange("p c j w -> p c (j w)"),
+                in_=rows.rearrange("(c p j) w -> p c (j w)", p=P, j=4),
+            )
 
         for s in range(4):
-            load_x(0, s)
+            load_x(0, s, 1)
             if s == 0:
                 nc.sync.dma_start(out=ks_row[0:1, :], in_=k_scale.rearrange("(o d) -> o d", o=1))
-            load_w("v", s)
+            load_w("v", s, 1)
         nc.sync.dma_start(out=cos_sb[:], in_=cos.rearrange("(p j) c -> p j c", j=J))
         nc.sync.dma_start(out=sin_sb[:], in_=sin.rearrange("(p j) c -> p j c", j=J))
-        for s in range(4):
-            load_x(1, s)
-        for s in range(4):
-            load_w("k", s)
+        load_x(1, 0, 4)
+        load_w("k", 0, 4)
 
         def transpose_x(b, j):
-            words = x_raw[b, j][:].bitcast(F32)
+            words = x_raw[b][:, j, :].bitcast(F32)
             banks = []
             for h in range(2):
                 xt = psum.tile([P, 4, P], F32, name="xt%d%d%d" % (b, j, h), tag="xt")
@@ -122,7 +125,7 @@ def tile_multiheadattention_pb_kernel(tc, kv_input, Wk, Wv, k_scale, cos, sin, o
         def copy_w(m, c):
             grp = work.tile([P, NW, 4], BF16, name="w_grp%s%d" % (m, c), tag="w_grp", align_bytes=64)
             dst = grp[:].rearrange("p (c i) j -> p c j i", i=4)
-            src = w_raw[m, c][:].rearrange("p j (c i) -> p c j i", i=4)
+            src = w_raw[m][:, c, :, :].rearrange("p j (c i) -> p c j i", i=4)
             cut = W_SPLIT[m] // 4
             nc.vector.tensor_copy(out=dst[:, :cut], in_=src[:, :cut])
             nc.scalar.copy(out=dst[:, cut:], in_=src[:, cut:])

@@ -39,20 +39,20 @@ def tile_multiheadattention_pb_kernel(tc, kv_input, Wk, Wv, k_scale, cos, sin, o
 
         x_raw, x_codes, x_scales = {}, {}, {}
         for b in range(B):
-            x_raw[b] = keep.tile([P, J, D], BF16, name="x_raw%d" % b)
+            x_raw[b] = keep.tile([P, J, D], BF16, name="x_raw%d" % b, align_bytes=256)
             for j in range(J):
                 x_codes[b, j] = keep.tile([P, NPASS * P], U32, name="x_codes%d%d" % (b, j), align_bytes=64)
                 x_scales[b, j] = keep.tile([P, NPASS * P], U8, name="x_scales%d%d" % (b, j), align_bytes=64)
         w_raw, w_codes, w_scales = {}, {}, {}
         for m in ("v", "k"):
-            w_raw[m] = keep.tile([P, NPASS, 4, NW], BF16, name="w_raw%s" % m)
+            w_raw[m] = keep.tile([P, NPASS, 4, NW], BF16, name="w_raw%s" % m, align_bytes=256)
             for c in range(NPASS):
                 w_codes[m, c] = keep.tile([P, NW], U32, name="w_codes%s%d" % (m, c), align_bytes=64)
                 w_scales[m, c] = keep.tile([P, NW], U8, name="w_scales%s%d" % (m, c), align_bytes=64)
         v_sb, k_sb = {}, {}
         for b in range(B):
-            v_sb[b] = keep.tile([P, G, J * HD], F32, name="v_sb%d" % b)
-            k_sb[b] = keep.tile([P, G, J * HD], F32, name="k_sb%d" % b)
+            v_sb[b] = keep.tile([P, G, J * HD], F32, name="v_sb%d" % b, align_bytes=256)
+            k_sb[b] = keep.tile([P, G, J * HD], F32, name="k_sb%d" % b, align_bytes=256)
 
         one_col = keep.tile([P, 1], F32, name="one_col")
         eps_col = keep.tile([P, 1], F32, name="eps_col")
@@ -60,8 +60,8 @@ def tile_multiheadattention_pb_kernel(tc, kv_input, Wk, Wv, k_scale, cos, sin, o
         ones = keep.tile([P, NW], BF16, name="ones")
         ks_row = keep.tile([P, HD], BF16, name="ks_row")
         ident = keep.tile([P, P], F32, name="ident")
-        cos_sb = keep.tile([P, J, HALF], BF16, name="cos_sb")
-        sin_sb = keep.tile([P, J, HALF], BF16, name="sin_sb")
+        cos_sb = keep.tile([P, J, HALF], BF16, name="cos_sb", align_bytes=256)
+        sin_sb = keep.tile([P, J, HALF], BF16, name="sin_sb", align_bytes=256)
         gain = keep.tile([P, HD], F32, name="gain")
         gain_s = keep.tile([P, HD], F32, name="gain_s")
         tab_a = keep.tile([P, J, HD], F32, name="tab_a")

@@ -23,6 +23,7 @@ NW = G * HD
 W_SPLIT = {"v": 336, "k": 336}
 V_ON_VECTOR = ((0, 0), (0, 2), (1, 2))
 N_WARM = 4
+BIG = 4096
 
 FLOPS = 2 * B * T * D * 2 * NW
 
@@ -39,20 +40,20 @@ def tile_multiheadattention_pb_kernel(tc, kv_input, Wk, Wv, k_scale, cos, sin, o
 
         x_raw, x_codes, x_scales = {}, {}, {}
         for b in range(B):
-            x_raw[b] = keep.tile([P, J, D], BF16, name="x_raw%d" % b, align_bytes=256)
+            x_raw[b] = keep.tile([P, J, D], BF16, name="x_raw%d" % b, align_bytes=BIG)
             for j in range(J):
                 x_codes[b, j] = keep.tile([P, NPASS * P], U32, name="x_codes%d%d" % (b, j), align_bytes=64)
                 x_scales[b, j] = keep.tile([P, NPASS * P], U8, name="x_scales%d%d" % (b, j), align_bytes=64)
         w_raw, w_codes, w_scales = {}, {}, {}
         for m in ("v", "k"):
-            w_raw[m] = keep.tile([P, NPASS, 4, NW], BF16, name="w_raw%s" % m, align_bytes=256)
+            w_raw[m] = keep.tile([P, NPASS, 4, NW], BF16, name="w_raw%s" % m, align_bytes=BIG)
             for c in range(NPASS):
                 w_codes[m, c] = keep.tile([P, NW], U32, name="w_codes%s%d" % (m, c), align_bytes=64)
                 w_scales[m, c] = keep.tile([P, NW], U8, name="w_scales%s%d" % (m, c), align_bytes=64)
         v_sb, k_sb = {}, {}
         for b in range(B):
-            v_sb[b] = keep.tile([P, G, J * HD], F32, name="v_sb%d" % b, align_bytes=256)
-            k_sb[b] = keep.tile([P, G, J * HD], F32, name="k_sb%d" % b, align_bytes=256)
+            v_sb[b] = keep.tile([P, G, J * HD], F32, name="v_sb%d" % b, align_bytes=BIG)
+            k_sb[b] = keep.tile([P, G, J * HD], F32, name="k_sb%d" % b, align_bytes=BIG)
 
         one_col = keep.tile([P, 1], F32, name="one_col")
         eps_col = keep.tile([P, 1], F32, name="eps_col")
@@ -60,8 +61,8 @@ def tile_multiheadattention_pb_kernel(tc, kv_input, Wk, Wv, k_scale, cos, sin, o
         ones = keep.tile([P, NW], BF16, name="ones")
         ks_row = keep.tile([P, HD], BF16, name="ks_row")
         ident = keep.tile([P, P], F32, name="ident")
-        cos_sb = keep.tile([P, J, HALF], BF16, name="cos_sb", align_bytes=256)
-        sin_sb = keep.tile([P, J, HALF], BF16, name="sin_sb", align_bytes=256)
+        cos_sb = keep.tile([P, J, HALF], BF16, name="cos_sb", align_bytes=512)
+        sin_sb = keep.tile([P, J, HALF], BF16, name="sin_sb", align_bytes=512)
         gain = keep.tile([P, HD], F32, name="gain")
         gain_s = keep.tile([P, HD], F32, name="gain_s")
         tab_a = keep.tile([P, J, HD], F32, name="tab_a")

from contextlib import ExitStack

import concourse.mybir as mybir
from concourse.masks import make_identity

F32 = mybir.dt.float32
BF16 = mybir.dt.bfloat16
U32 = mybir.dt.uint32
U8 = mybir.dt.uint8
E5X4 = mybir.dt.float8_e5m2_x4
ACT = mybir.ActivationFunctionType
ALU = mybir.AluOpType

B, T, D = 2, 512, 2048
G, HD, R = 4, 128, 4
HALF = HD // 2
EPS = 1e-6
P = 128
J = T // P
K_PASS = 4 * P
NPASS = D // K_PASS
NW = G * HD
W_SPLIT = {"v": 336, "k": 336}
V_ON_VECTOR = ((0, 0), (0, 2), (1, 2))
N_WARM = 4
BIG = 4096

FLOPS = 2 * B * T * D * 2 * NW


def tile_multiheadattention_pb_kernel(tc, kv_input, Wk, Wv, k_scale, cos, sin, out_0, out_1):
    nc = tc.nc
    weights = {"k": Wk, "v": Wv}

    with ExitStack() as ctx:
        keep = ctx.enter_context(tc.tile_pool(name="keep", bufs=1))
        work = ctx.enter_context(tc.tile_pool(name="work", bufs=3))
        psum = ctx.enter_context(tc.psum_pool(name="psum", bufs=4))
        ctx.enter_context(tc.manual_schedule())

        x_raw, x_codes, x_scales = {}, {}, {}
        for b in range(B):
            x_raw[b] = keep.tile([P, J, D], BF16, name="x_raw%d" % b, align_bytes=BIG)
            for j in range(J):
                x_codes[b, j] = keep.tile([P, NPASS * P], U32, name="x_codes%d%d" % (b, j), align_bytes=64)
                x_scales[b, j] = keep.tile([P, NPASS * P], U8, name="x_scales%d%d" % (b, j), align_bytes=64)
        w_raw, w_codes, w_scales = {}, {}, {}
        for m in ("v", "k"):
            w_raw[m] = keep.tile([P, NPASS, 4, NW], BF16, name="w_raw%s" % m, align_bytes=BIG)
            for c in range(NPASS):
                w_codes[m, c] = keep.tile([P, NW], U32, name="w_codes%s%d" % (m, c), align_bytes=64)
                w_scales[m, c] = keep.tile([P, NW], U8, name="w_scales%s%d" % (m, c), align_bytes=64)
        v_sb, k_sb = {}, {}
        for b in range(B):
            v_sb[b] = keep.tile([P, G, J * HD], F32, name="v_sb%d" % b, align_bytes=BIG)
            k_sb[b] = keep.tile([P, G, J * HD], F32, name="k_sb%d" % b, align_bytes=BIG)

        one_col = keep.tile([P, 1], F32, name="one_col")
        eps_col = keep.tile([P, 1], F32, name="eps_col")
        warm = keep.tile([P, 1], F32, name="warm")
        ones = keep.tile([P, NW], BF16, name="ones")
        ks_row = keep.tile([P, HD], BF16, name="ks_row")
        ident = keep.tile([P, P], F32, name="ident")
        cos_sb = keep.tile([P, J, HALF], BF16, name="cos_sb", align_bytes=512)
        sin_sb = keep.tile([P, J, HALF], BF16, name="sin_sb", align_bytes=512)
        gain = keep.tile([P, HD], F32, name="gain")
        gain_s = keep.tile([P, HD], F32, name="gain_s")
        tab_a = keep.tile([P, J, HD], F32, name="tab_a")
        tab_b = keep.tile([P, J, HD], F32, name="tab_b")

        nc.vector.memset(ones[:], 1.0)
        nc.vector.memset(ks_row[:], 0.0)
        nc.vector.memset(one_col[:], 1.0)
        nc.scalar.activation(out=warm[:], in_=one_col[:], func=ACT.Sqrt)
        make_identity(nc, ident[:])
        nc.vector.tensor_scalar(out=eps_col[:], in0=one_col[:], scalar1=0.0, scalar2=EPS, op0=ALU.mult, op1=ALU.add)

        def load_x(b, j, n):
            nc.sync.dma_start(
                out=x_raw[b][:, j : j + n, :], in_=kv_input[b].rearrange("(p j) k -> p j k", j=J)[:, j : j + n, :]
            )

        def load_w(m, c, n):
            rows = weights[m][c * K_PASS : (c + n) * K_PASS, :]
            nc.sync.dma_start(
                out=w_raw[m][:, c : c + n, :, :].rearrange("p c j w -> p c (j w)"),
                in_=rows.rearrange("(c p j) w -> p c (j w)", p=P, j=4),
            )

        for s in range(4):
            load_x(0, s, 1)
            if s == 0:
                nc.sync.dma_start(out=ks_row[0:1, :], in_=k_scale.rearrange("(o d) -> o d", o=1))
            load_w("v", s, 1)
        nc.sync.dma_start(out=cos_sb[:], in_=cos.rearrange("(p j) c -> p j c", j=J))
        nc.sync.dma_start(out=sin_sb[:], in_=sin.rearrange("(p j) c -> p j c", j=J))
        load_x(1, 0, 4)
        load_w("k", 0, 4)

        def transpose_x(b, j):
            words = x_raw[b][:, j, :].bitcast(F32)
            banks = []
            for h in range(2):
                xt = psum.tile([P, 4, P], F32, name="xt%d%d%d" % (b, j, h), tag="xt")
                for i in range(4):
                    c, u = 2 * h + i // 2, i % 2
                    nc.tensor.transpose(
                        out=xt[:, i, :], in_=words[:, 256 * c + u : 256 * (c + 1) : 2], identity=ident[:]
                    )
                banks.append(xt)
            return banks

        def copy_x(b, j, banks):
            grp = work.tile([P, D], BF16, name="x_grp%d%d" % (b, j), tag="x_grp", align_bytes=64)
            grp_words = grp[:].bitcast(F32)
            for h in range(2):
                nc.scalar.copy(
                    out=grp_words[:, 512 * h : 512 * (h + 1)].rearrange("p (c r u) -> p c r u", c=2, u=2),
                    in_=banks[h][:].rearrange("p (c u) r -> p c r u", u=2),
                )
            return grp

        def quantize_x(b, j, grp):
            nc.vector.quantize_mx(out=x_codes[b, j][:].bitcast(E5X4), scales=x_scales[b, j][:], in_=grp[:])

        def copy_w(m, c):
            grp = work.tile([P, NW, 4], BF16, name="w_grp%s%d" % (m, c), tag="w_grp", align_bytes=64)
            dst = grp[:].rearrange("p (c i) j -> p c j i", i=4)
            src = w_raw[m][:, c, :, :].rearrange("p j (c i) -> p c j i", i=4)
            cut = W_SPLIT[m] // 4
            nc.vector.tensor_copy(out=dst[:, :cut], in_=src[:, :cut])
            nc.scalar.copy(out=dst[:, cut:], in_=src[:, cut:])
            return grp

        def quantize_w(m, c, grp):
            nc.vector.quantize_mx(
                out=w_codes[m, c][:].bitcast(E5X4),
                scales=w_scales[m, c][:],
                in_=grp[:].rearrange("p w j -> p (w j)"),
            )

        def mm(acc, m, b, j, c):
            cols = slice(c * P, (c + 1) * P)
            nc.tensor.matmul_mx(
                out=acc[:],
                lhsT=x_codes[b, j][:, cols].bitcast(E5X4),
                lhsT_scale=x_scales[b, j][:, cols],
                rhs=w_codes[m, c][:].bitcast(E5X4),
                rhs_scale=w_scales[m, c][:],
                start=(c == 0),
                stop=(c == NPASS - 1),
            )

        def evacuate_v(acc, b, j):
            dst = v_sb[b][:, :, j * HD : (j + 1) * HD]
            src = acc[:].rearrange("p (g d) -> p g d", g=G)
            if (b, j) in V_ON_VECTOR:
                nc.vector.tensor_copy(out=dst, in_=src)
            else:
                nc.scalar.copy(out=dst, in_=src)

        def store_v(b):
            view = out_1[b].rearrange("(g r) (p j) d -> r p g (j d)", r=R, j=J)
            for r in range(R):
                nc.sync.dma_start(out=view[r], in_=v_sb[b][:])

        def store_k(b, g):
            heads = out_0[b, g * R : (g + 1) * R].rearrange("r (p j) d -> p r (j d)", j=J)
            nc.sync.dma_start(out=heads, in_=k_sb[b][:, g, :].unsqueeze(1).to_broadcast([P, R, J * HD]))

        warm_ps = psum.tile([P, NW], F32, name="warm_ps", tag="acc")
        for i in range(N_WARM):
            nc.tensor.matmul(out=warm_ps[:], lhsT=ones[:, :P], rhs=ones[:], start=True, stop=True)
        ks_ps = psum.tile([P, NW], F32, name="ks_ps", tag="xt")
        nc.tensor.matmul(out=ks_ps[:, :HD], lhsT=ones[:, :P], rhs=ks_row[:], start=True, stop=True)
        nc.vector.tensor_scalar(out=gain[:], in0=ks_ps[:, :HD], scalar1=1.0, scalar2=None, op0=ALU.add)
        nc.vector.tensor_scalar(out=gain_s[:, :HALF], in0=ks_ps[:, :HALF], scalar1=1.0, scalar2=None, op0=ALU.add)
        nc.vector.tensor_scalar(
            out=gain_s[:, HALF:], in0=ks_ps[:, HALF:HD], scalar1=-1.0, scalar2=-1.0, op0=ALU.mult, op1=ALU.add
        )

        acc_v = {}
        banks = {}
        banks[0, 0] = transpose_x(0, 0)
        for s in range(4):
            x_grp = copy_x(0, s, banks[0, s])
            w_grp = copy_w("v", s)
            if s < 3:
                banks[0, s + 1] = transpose_x(0, s + 1)
            quantize_x(0, s, x_grp)
            quantize_w("v", s, w_grp)
            acc_v[0, s] = psum.tile([P, NW], F32, name="acc_v0%d" % s, tag="acc")
            for c in range(s):
                mm(acc_v[0, s], "v", 0, s, c)
            for j in range(s + 1):
                mm(acc_v[0, j], "v", 0, j, s)

        def mm_v1(s):
            acc_v[1, s] = psum.tile([P, NW], F32, name="acc_v1%d" % s, tag="acc")
            for c in range(NPASS):
                mm(acc_v[1, s], "v", 1, s, c)

        x_grps, w_grps = {}, {}
        banks[1, 0] = transpose_x(1, 0)
        banks[1, 1] = transpose_x(1, 1)
        for j in range(J):
            evacuate_v(acc_v[0, j], 0, j)
        store_v(0)
        x_grps[0] = copy_x(1, 0, banks[1, 0])

        for tab, gn, trig in ((tab_a, gain, cos_sb), (tab_b, gain_s, sin_sb)):
            nc.vector.tensor_tensor(
                out=tab[:].rearrange("p j (h c) -> p j h c", h=2),
                in0=gn[:].rearrange("p (h c) -> p h c", h=2).unsqueeze(1).to_broadcast([P, J, 2, HALF]),
                in1=trig[:].unsqueeze(2).to_broadcast([P, J, 2, HALF]),
                op=ALU.mult,
            )

        quantize_x(1, 0, x_grps[0])
        x_grps[1] = copy_x(1, 1, banks[1, 1])
        banks[1, 2] = transpose_x(1, 2)
        mm_v1(0)
        quantize_x(1, 1, x_grps[1])
        x_grps[2] = copy_x(1, 2, banks[1, 2])
        banks[1, 3] = transpose_x(1, 3)
        mm_v1(1)
        quantize_x(1, 2, x_grps[2])
        x_grps[3] = copy_x(1, 3, banks[1, 3])
        mm_v1(2)
        evacuate_v(acc_v[1, 0], 1, 0)
        w_grps[0] = copy_w("k", 0)
        quantize_x(1, 3, x_grps[3])
        mm_v1(3)
        evacuate_v(acc_v[1, 1], 1, 1)
        w_grps[1] = copy_w("k", 1)
        quantize_w("k", 0, w_grps[0])
        evacuate_v(acc_v[1, 2], 1, 2)
        evacuate_v(acc_v[1, 3], 1, 3)
        store_v(1)
        acc_k = {}
        for j in range(J):
            acc_k[0, j] = psum.tile([P, NW], F32, name="acc_k0%d" % j, tag="acc")
            mm(acc_k[0, j], "k", 0, j, 0)
        for c in range(1, NPASS):
            if c + 1 < NPASS:
                w_grps[c + 1] = copy_w("k", c + 1)
            quantize_w("k", c, w_grps[c])
            for j in range(J):
                mm(acc_k[0, j], "k", 0, j, c)
        for j in range(J):
            acc_k[1, j] = psum.tile([P, NW], F32, name="acc_k1%d" % j, tag="xt")

        rms, rstd, xn, yz = {}, {}, {}, {}

        def squares(u):
            b, g = u // G, u % G
            ss = work.tile([P, J], F32, name="ss%d" % u, tag="ss", bufs=4)
            rms[u] = work.tile([P, J], F32, name="rms%d" % u, tag="rms", bufs=4)
            for j in range(J):
                junk = work.tile([P, HD], BF16, name="junk%d%d" % (u, j), tag="junk", bufs=2)
                nc.scalar.activation(
                    out=junk[:],
                    in_=acc_k[b, j][:, g * HD : (g + 1) * HD],
                    func=ACT.Square,
                    accum_out=ss[:, j : j + 1],
                )
            nc.scalar.activation(out=rms[u][:], in_=ss[:], func=ACT.Sqrt, bias=eps_col[:], scale=1.0 / HD)

        def recip(u):
            rstd[u] = work.tile([P, J], F32, name="rstd%d" % u, tag="rstd", bufs=4)
            nc.vector.reciprocal(out=rstd[u][:], in_=rms[u][:])

        def normalise(u):
            b, g = u // G, u % G
            xn[u] = work.tile([P, J, HD], F32, name="xn%d" % u, tag="xn")
            for j in range(J):
                nc.scalar.activation(
                    out=xn[u][:, j, :],
                    in_=acc_k[b, j][:, g * HD : (g + 1) * HD],
                    func=ACT.Copy,
                    scale=rstd[u][:, j : j + 1],
                )

        def rope_mul(u):
            y = work.tile([P, J, HD], F32, name="y%d" % u, tag="y")
            z = work.tile([P, J, HD], F32, name="z%d" % u, tag="z")
            nc.vector.tensor_tensor(out=y[:], in0=xn[u][:], in1=tab_a[:], op=ALU.mult)
            nc.vector.tensor_tensor(out=z[:], in0=xn[u][:], in1=tab_b[:], op=ALU.mult)
            yz[u] = (y, z)

        def rope_add(u):
            b, g = u // G, u % G
            y, z = yz[u]
            dst = k_sb[b][:, g, :].rearrange("p (j d) -> p j d", j=J)
            nc.vector.tensor_tensor(out=dst[:, :, :HALF], in0=y[:, :, :HALF], in1=z[:, :, HALF:], op=ALU.add)
            nc.vector.tensor_tensor(out=dst[:, :, HALF:], in0=y[:, :, HALF:], in1=z[:, :, :HALF], op=ALU.add)
            store_k(b, g)

        squares(0)
        recip(0)
        for j in range(J):
            for c in range(NPASS):
                mm(acc_k[1, j], "k", 1, j, c)
        normalise(0)
        squares(1)
        squares(2)
        rope_mul(0)
        recip(1)
        rope_add(0)
        recip(2)
        normalise(1)
        for u in range(1, B * G):
            if u + 2 < B * G:
                squares(u + 2)
            if u + 1 < B * G:
                normalise(u + 1)
            rope_mul(u)
            if u + 2 < B * G:
                recip(u + 2)
            rope_add(u)
